import numpy as np
import ml_dtypes


def mxq(x, axis, fmt="e4m3"):
    dtype, down = {"e4m3": (ml_dtypes.float8_e4m3fn, 7), "e5m2": (ml_dtypes.float8_e5m2, 14)}[fmt]
    v = np.moveaxis(np.asarray(x, np.float32).astype(ml_dtypes.bfloat16).astype(np.float64), axis, -1)
    blocks = v.reshape(v.shape[:-1] + (-1, 32))
    amax = np.abs(blocks).max(-1, keepdims=True)
    byte = np.maximum(np.where(amax > 0, np.frexp(amax)[1] - 1 + 127, 0) - down, 1)
    scale = np.exp2(byte - 127.0)
    codes = (blocks / scale).astype(np.float32).astype(dtype).astype(np.float64)
    return np.moveaxis((codes * scale).reshape(v.shape), -1, axis)


WIDE = False


def mx_kscale(k):
    if not WIDE:
        return np.ones(k)
    levels = np.array([10, -10, 5, -5, 0])
    if k % 512:
        return np.exp2(np.random.permutation(np.resize(levels, k // 32))).repeat(32)
    a = np.empty((k // 512, 16))
    for p in range(k // 512):
        a[p, :8] = np.random.permutation(np.resize(levels, 8))
        for g in range(8):
            far = levels[np.abs(levels - a[p, g]) >= 10]
            a[p, g + 8] = far[np.random.randint(len(far))]
    return np.exp2(a.ravel()).repeat(32)


BF16 = ml_dtypes.bfloat16


def bf(x):
    return np.asarray(x, np.float32).astype(BF16)


def f64(x):
    return np.asarray(x).astype(np.float64)


N, H, W, K = 512, 2048, 8, 512
TAU = 1.0


def silu(v):
    return v / (1.0 + np.exp(-v))


def softmax_last(v):
    e = np.exp(v - v.max(-1, keepdims=True))
    return e / e.sum(-1, keepdims=True)


def setup_inputs():
    s = np.tile(mx_kscale(K), W)
    return {"x": bf(np.random.standard_normal((N, W * K)) * s),
            "template_flat": bf(np.random.standard_normal((H, W * K)) / np.sqrt(K) / s)}


def reference(x, template_flat):
    n = x.shape[0]
    h = template_flat.shape[0]
    xw = f64(x).reshape(n, W, K)
    tw = f64(template_flat).reshape(h, W, K)
    xq = mxq(xw, 2, "e4m3")
    tq = mxq(tw, 2, "e4m3")
    s = (xq.transpose(1, 0, 2) @ tq.transpose(1, 2, 0)).transpose(1, 2, 0)
    gate = softmax_last(s / TAU)
    return np.sum(gate * silu(s), axis=-1)

@@ -1,0 +1,219 @@
+from contextlib import ExitStack
+
+import concourse.mybir as mybir
+from concourse.masks import make_identity
+
+FP8X4 = mybir.dt.float8_e4m3fn_x4
+BF16 = mybir.dt.bfloat16
+F32 = mybir.dt.float32
+U32 = mybir.dt.uint32
+U8 = mybir.dt.uint8
+ACT = mybir.ActivationFunctionType
+ALU = mybir.AluOpType
+
+P = 128
+N, H, W, K = 512, 2048, 8, 512
+FLOPS = 2 * N * H * W * K
+
+NC = 256
+ROUNDS = (H // P) * (N // NC)
+BANKS = 4
+PINNED = False
+
+
+def tile_dendriticlayersilu_ffn_kernel(tc, x, template_flat, out):
+    nc = tc.nc
+    with ExitStack() as ctx:
+        if PINNED:
+            ctx.enter_context(tc.manual_schedule())
+        const = ctx.enter_context(tc.tile_pool(name="const", bufs=1))
+        raw_pool = ctx.enter_context(tc.tile_pool(name="raw", bufs=6))
+        grp_pool = ctx.enter_context(tc.tile_pool(name="grp", bufs=2))
+        tq_pool = ctx.enter_context(tc.tile_pool(name="tq", bufs=3))
+        t_pool = ctx.enter_context(tc.tile_pool(name="tanh", bufs=6))
+        u_pool = ctx.enter_context(tc.tile_pool(name="u", bufs=12))
+        y_pool = ctx.enter_context(tc.tile_pool(name="y", bufs=12))
+        m_pool = ctx.enter_context(tc.tile_pool(name="m", bufs=2))
+        ps_s = ctx.enter_context(tc.psum_pool(name="ps_s", bufs=5))
+        ps_za = ctx.enter_context(tc.psum_pool(name="ps_za", bufs=1))
+        ps_tp = ctx.enter_context(tc.psum_pool(name="ps_tp", bufs=2))
+
+        ident = const.tile([P, P], F32, name="ident")
+        make_identity(nc, ident[:])
+        xq = const.tile([P, W * N], U32, name="xq", align_bytes=64)
+        xs = const.tile([P, W * N], U8, name="xs", align_bytes=64)
+        out_sb = const.tile([P, N // P, H], F32, name="out_sb")
+
+        blocks = [("x", 0), ("x", 1), ("t", 0), ("x", 2), ("x", 3)] + [("t", i) for i in range(1, H // P)]
+        raw = {}
+        grp = {}
+        tq = {}
+        ts = {}
+
+        def load(i):
+            kind, idx = blocks[i]
+            src = x if kind == "x" else template_flat
+            r = raw_pool.tile([P, W * K], BF16, name="raw")
+            nc.sync.dma_start(out=r[:], in_=src[idx * P : (idx + 1) * P, :])
+            raw[i] = r
+
+        def transposes(i, j, engine):
+            if j == 0:
+                grp[i] = grp_pool.tile([P, W * K], BF16, name="grp", align_bytes=64)
+            words = raw[i][:].bitcast(F32)
+            tp = ps_tp.tile([P, 512], F32, name="tp")
+            for q in range(4):
+                first = (2 * j + q // 2) * 2 * P + q % 2
+                nc.tensor.transpose(tp[:, q * P : (q + 1) * P], words[:, first : first + 2 * P - 1 : 2], ident[:])
+            dst = grp[i][:].bitcast(F32)[:, j * 512 : (j + 1) * 512].rearrange("p (a r u) -> p a r u", a=2, u=2)
+            src = tp[:].rearrange("p (a u r) -> p a r u", a=2, u=2)
+            if engine == "scalar":
+                nc.scalar.copy(out=dst, in_=src)
+            else:
+                nc.vector.tensor_copy(out=dst, in_=src)
+
+        def quantise(i):
+            kind, idx = blocks[i]
+            g = grp[i]
+            if kind == "x":
+                for w in range(W):
+                    cols = slice(w * N + idx * P, w * N + (idx + 1) * P)
+                    nc.vector.quantize_mx(out=xq[:, cols].bitcast(FP8X4), scales=xs[:, cols], in_=g[:, w * 512 : (w + 1) * 512])
+            else:
+                q = tq_pool.tile([P, W * P], U32, name="tq", align_bytes=64)
+                s = tq_pool.tile([P, W * P], U8, name="ts", align_bytes=64)
+                nc.vector.quantize_mx(out=q[:].bitcast(FP8X4), scales=s[:], in_=g[:])
+                tq[idx] = q
+                ts[idx] = s
+
+        s_ps = {}
+        c0 = {}
+        tanh = {}
+        yv = {}
+        du = {}
+        mx = {}
+        mm = {}
+        za = {}
+
+        def fill(r, b):
+            hb, c = r // 2, r % 2
+            s = ps_s.tile([P, 512], F32, name="s")
+            for a in range(2):
+                w = 2 * b + a
+                nc.tensor.matmul_mx(
+                    out=s[:, a * NC : (a + 1) * NC],
+                    lhsT=tq[hb][:, w * P : (w + 1) * P].bitcast(FP8X4),
+                    lhsT_scale=ts[hb][:, w * P : (w + 1) * P],
+                    rhs=xq[:, w * N + c * NC : w * N + (c + 1) * NC].bitcast(FP8X4),
+                    rhs_scale=xs[:, w * N + c * NC : w * N + (c + 1) * NC],
+                    start=True,
+                    stop=True,
+                )
+            s_ps[(r, b)] = s
+            if b == 0:
+                cp = m_pool.tile([P, 512], F32, name="c0")
+                nc.scalar.copy(out=cp[:], in_=s[:])
+                c0[r] = cp
+            t = t_pool.tile([P, 512], F32, name="tanh")
+            nc.scalar.activation(out=t[:], in_=s[:], func=ACT.Tanh, scale=0.5)
+            tanh[(r, b)] = t
+
+        def gate_and_max(r, b):
+            s = s_ps[(r, b)]
+            y = y_pool.tile([P, 512], F32, name="y")
+            nc.vector.scalar_tensor_tensor(out=y[:], in0=tanh[(r, b)][:], scalar=1.0, in1=s[:], op0=ALU.add, op1=ALU.mult)
+            yv[(r, b)] = y
+            if b == 1:
+                mx[r] = m_pool.tile([P, 512], F32, name="mx")
+                nc.vector.tensor_tensor(out=mx[r][:], in0=s[:], in1=c0[r][:], op=ALU.max)
+            elif b > 1:
+                nc.vector.tensor_tensor(out=mx[r][:], in0=s[:], in1=mx[r][:], op=ALU.max)
+            if b == BANKS - 1:
+                mm[r] = m_pool.tile([P, NC], F32, name="mm")
+                nc.vector.tensor_tensor(out=mm[r][:], in0=mx[r][:, 0:NC], in1=mx[r][:, NC : 2 * NC], op=ALU.max)
+
+        def weights(r, b):
+            s = s_ps[(r, b)]
+            d = u_pool.tile([P, 512], F32, name="u")
+            nc.vector.tensor_tensor(
+                out=d[:].rearrange("p (a n) -> p a n", a=2),
+                in0=s[:].rearrange("p (a n) -> p a n", a=2),
+                in1=mm[r][:].unsqueeze(1).to_broadcast([P, 2, NC]),
+                op=ALU.subtract,
+            )
+            nc.scalar.activation(out=d[:], in_=d[:], func=ACT.Exp)
+            du[(r, b)] = d
+            y = yv[(r, b)]
+            nc.gpsimd.tensor_tensor(out=y[:], in0=y[:], in1=d[:], op=ALU.mult)
+
+        def sums(r):
+            z = ps_za.tile([P, 512], F32, name="za")
+            for slot in range(4):
+                src = du if slot < 2 else yv
+                nb = slot % 2
+                for w in range(W):
+                    nc.tensor.matmul(
+                        out=z[:, slot * P : (slot + 1) * P],
+                        lhsT=src[(r, w // 2)][:, (w % 2) * NC + nb * P : (w % 2) * NC + (nb + 1) * P],
+                        rhs=ident[:],
+                        is_transpose=True,
+                        start=(w == 0),
+                        stop=(w == W - 1),
+                    )
+            za[r] = z
+
+        def finish(r):
+            hb, c = r // 2, r % 2
+            z = za[r]
+            rz = m_pool.tile([P, NC], F32, name="rz")
+            nc.vector.reciprocal(out=rz[:], in_=z[:, 0:NC])
+            nc.vector.scalar_tensor_tensor(
+                out=out_sb[:, 2 * c : 2 * c + 2, hb * P : (hb + 1) * P],
+                in0=z[:, NC : 2 * NC].rearrange("p (a h) -> p a h", a=2),
+                scalar=0.5,
+                in1=rz[:].rearrange("p (a h) -> p a h", a=2),
+                op0=ALU.mult,
+                op1=ALU.mult,
+            )
+            if hb % 4 == 3 and c == 1:
+                cols = slice((hb - 3) * P, (hb + 1) * P)
+                for nb in range(N // P):
+                    nc.sync.dma_start(out=out[nb * P : (nb + 1) * P, cols], in_=out_sb[:, nb, cols])
+
+        HEAD = 6
+        for i in range(HEAD):
+            load(i)
+        for i in range(HEAD):
+            for j in range(4):
+                transposes(i, j, "scalar" if j % 2 == 0 else "vector")
+            load(i + HEAD)
+            if i > 0:
+                quantise(i - 1)
+        quantise(HEAD - 1)
+
+        for r in range(-1, ROUNDS + 1):
+            nxt = r + 1 < ROUNDS
+            if nxt:
+                fill(r + 1, 0)
+            hb_t = (r + 4) // 2
+            i_t = hb_t + 4
+            if r >= 0 and hb_t < H // P:
+                for j in range(2):
+                    transposes(i_t, 2 * (r % 2) + j, "scalar")
+                if r % 2 == 1 and i_t + HEAD < len(blocks):
+                    load(i_t + HEAD)
+            if 0 <= r < ROUNDS:
+                for b in range(BANKS):
+                    gate_and_max(r, b)
+            if r >= 1:
+                sums(r - 1)
+            for b in range(BANKS):
+                if 0 <= r < ROUNDS:
+                    weights(r, b)
+                if nxt and b < BANKS - 1:
+                    fill(r + 1, b + 1)
+            if r >= 1:
+                finish(r - 1)
+            hb_q = (r + 2) // 2
+            if r >= 2 and r % 2 == 0 and hb_q < H // P:
+                quantise(hb_q + 4)

@@ -10,41 +10,44 @@ U32 = mybir.dt.uint32
 U8 = mybir.dt.uint8
 ACT = mybir.ActivationFunctionType
 ALU = mybir.AluOpType
+AX = mybir.AxisListType
 
 P = 128
 N, H, W, K = 512, 2048, 8, 512
 FLOPS = 2 * N * H * W * K
 
 NC = 256
-ROUNDS = (H // P) * (N // NC)
 BANKS = 4
-PINNED = False
+B = 512
+BATCHES = 8
+COLS = 2 * P
 
 
 def tile_dendriticlayersilu_ffn_kernel(tc, x, template_flat, out):
     nc = tc.nc
     with ExitStack() as ctx:
-        if PINNED:
-            ctx.enter_context(tc.manual_schedule())
+        ctx.enter_context(tc.manual_schedule())
         const = ctx.enter_context(tc.tile_pool(name="const", bufs=1))
-        raw_pool = ctx.enter_context(tc.tile_pool(name="raw", bufs=6))
+        raw_pool = ctx.enter_context(tc.tile_pool(name="raw", bufs=3))
         grp_pool = ctx.enter_context(tc.tile_pool(name="grp", bufs=2))
-        tq_pool = ctx.enter_context(tc.tile_pool(name="tq", bufs=3))
-        t_pool = ctx.enter_context(tc.tile_pool(name="tanh", bufs=6))
-        u_pool = ctx.enter_context(tc.tile_pool(name="u", bufs=12))
-        y_pool = ctx.enter_context(tc.tile_pool(name="y", bufs=12))
-        m_pool = ctx.enter_context(tc.tile_pool(name="m", bufs=2))
+        tq_pool = ctx.enter_context(tc.tile_pool(name="tq", bufs=4))
+        c_pool = ctx.enter_context(tc.tile_pool(name="c", bufs=4))
+        d_pool = ctx.enter_context(tc.tile_pool(name="d", bufs=8))
+        y_pool = ctx.enter_context(tc.tile_pool(name="y", bufs=8))
+        m_pool = ctx.enter_context(tc.tile_pool(name="m", bufs=4))
+        o_pool = ctx.enter_context(tc.tile_pool(name="o", bufs=2))
         ps_s = ctx.enter_context(tc.psum_pool(name="ps_s", bufs=5))
-        ps_za = ctx.enter_context(tc.psum_pool(name="ps_za", bufs=1))
-        ps_tp = ctx.enter_context(tc.psum_pool(name="ps_tp", bufs=2))
+        ps_t = ctx.enter_context(tc.psum_pool(name="ps_t", bufs=3))
 
         ident = const.tile([P, P], F32, name="ident")
         make_identity(nc, ident[:])
+        warm = const.tile([P, 1], F32, name="warm")
+        nc.scalar.activation(out=warm[:], in_=ident[:, 0:1], func=ACT.Silu)
         xq = const.tile([P, W * N], U32, name="xq", align_bytes=64)
         xs = const.tile([P, W * N], U8, name="xs", align_bytes=64)
-        out_sb = const.tile([P, N // P, H], F32, name="out_sb")
 
-        blocks = [("x", 0), ("x", 1), ("t", 0), ("x", 2), ("x", 3)] + [("t", i) for i in range(1, H // P)]
+        blocks = [("x", 0), ("x", 1), ("t", 0), ("t", 1), ("x", 2), ("x", 3)] + [("t", i) for i in range(2, H // P)]
+        index = {block: i for i, block in enumerate(blocks)}
         raw = {}
         grp = {}
         tq = {}
@@ -61,11 +64,11 @@ def tile_dendriticlayersilu_ffn_kernel(tc, x, template_flat, out):
             if j == 0:
                 grp[i] = grp_pool.tile([P, W * K], BF16, name="grp", align_bytes=64)
             words = raw[i][:].bitcast(F32)
-            tp = ps_tp.tile([P, 512], F32, name="tp")
+            tp = ps_t.tile([P, B], F32, name="t")
             for q in range(4):
                 first = (2 * j + q // 2) * 2 * P + q % 2
                 nc.tensor.transpose(tp[:, q * P : (q + 1) * P], words[:, first : first + 2 * P - 1 : 2], ident[:])
-            dst = grp[i][:].bitcast(F32)[:, j * 512 : (j + 1) * 512].rearrange("p (a r u) -> p a r u", a=2, u=2)
+            dst = grp[i][:].bitcast(F32)[:, j * B : (j + 1) * B].rearrange("p (a r u) -> p a r u", a=2, u=2)
             src = tp[:].rearrange("p (a u r) -> p a r u", a=2, u=2)
             if engine == "scalar":
                 nc.scalar.copy(out=dst, in_=src)
@@ -78,7 +81,7 @@ def tile_dendriticlayersilu_ffn_kernel(tc, x, template_flat, out):
             if kind == "x":
                 for w in range(W):
                     cols = slice(w * N + idx * P, w * N + (idx + 1) * P)
-                    nc.vector.quantize_mx(out=xq[:, cols].bitcast(FP8X4), scales=xs[:, cols], in_=g[:, w * 512 : (w + 1) * 512])
+                    nc.vector.quantize_mx(out=xq[:, cols].bitcast(FP8X4), scales=xs[:, cols], in_=g[:, w * K : (w + 1) * K])
             else:
                 q = tq_pool.tile([P, W * P], U32, name="tq", align_bytes=64)
                 s = tq_pool.tile([P, W * P], U8, name="ts", align_bytes=64)
@@ -86,134 +89,151 @@ def tile_dendriticlayersilu_ffn_kernel(tc, x, template_flat, out):
                 tq[idx] = q
                 ts[idx] = s
 
-        s_ps = {}
-        c0 = {}
-        tanh = {}
-        yv = {}
-        du = {}
-        mx = {}
-        mm = {}
-        za = {}
+        d_of = {}
+        y_of = {}
+        o_of = {}
 
-        def fill(r, b):
-            hb, c = r // 2, r % 2
-            s = ps_s.tile([P, 512], F32, name="s")
-            for a in range(2):
-                w = 2 * b + a
-                nc.tensor.matmul_mx(
-                    out=s[:, a * NC : (a + 1) * NC],
-                    lhsT=tq[hb][:, w * P : (w + 1) * P].bitcast(FP8X4),
-                    lhsT_scale=ts[hb][:, w * P : (w + 1) * P],
-                    rhs=xq[:, w * N + c * NC : w * N + (c + 1) * NC].bitcast(FP8X4),
-                    rhs_scale=xs[:, w * N + c * NC : w * N + (c + 1) * NC],
-                    start=True,
-                    stop=True,
+        s_of = {}
+        c_of = {}
+
+        def scores(hb, c):
+            banks = []
+            for b in range(BANKS):
+                s = ps_s.tile([P, B], F32, name="s")
+                for a in range(2):
+                    w = 2 * b + a
+                    cols = slice(w * N + c * NC, w * N + (c + 1) * NC)
+                    nc.tensor.matmul_mx(
+                        out=s[:, a * NC : (a + 1) * NC],
+                        lhsT=tq[hb][:, w * P : (w + 1) * P].bitcast(FP8X4),
+                        lhsT_scale=ts[hb][:, w * P : (w + 1) * P],
+                        rhs=xq[:, cols].bitcast(FP8X4),
+                        rhs_scale=xs[:, cols],
+                        start=True,
+                        stop=True,
+                    )
+                banks.append(s)
+                if b == 0:
+                    c0 = c_pool.tile([P, B], F32, name="c0")
+                    nc.scalar.copy(out=c0[:], in_=s[:])
+                    c_of[(hb, c)] = c0
+            s_of[(hb, c)] = banks
+
+        def silus(hb, c):
+            y = y_pool.tile([P, BANKS * B], F32, name="y")
+            y_of[(hb, c)] = y
+            for b in range(BANKS):
+                nc.scalar.activation(out=y[:, b * B : (b + 1) * B], in_=s_of[(hb, c)][b][:], func=ACT.Silu)
+
+        def shifts(hb, c):
+            banks = s_of[(hb, c)]
+            c0 = c_of[(hb, c)]
+            d = d_pool.tile([P, BANKS * B], F32, name="d")
+            d_of[(hb, c)] = d
+            mx = m_pool.tile([P, B], F32, name="mx", bufs=2)
+            nc.vector.tensor_tensor(out=mx[:], in0=banks[1][:], in1=c0[:], op=ALU.max)
+            for b in range(2, BANKS):
+                nc.vector.tensor_tensor(out=mx[:], in0=banks[b][:], in1=mx[:], op=ALU.max)
+            mm = m_pool.tile([P, NC], F32, name="mm")
+            nc.vector.tensor_reduce(out=mm[:], in_=mx[:].rearrange("p (a n) -> p n a", a=2), op=ALU.max, axis=AX.X)
+            for b in list(range(1, BANKS)) + [0]:
+                engine, source = (nc.gpsimd, c0) if b == 0 else (nc.vector, banks[b])
+                engine.tensor_tensor(
+                    out=d[:, b * B : (b + 1) * B].rearrange("p (a n) -> p a n", a=2),
+                    in0=source[:].rearrange("p (a n) -> p a n", a=2),
+                    in1=mm[:].unsqueeze(1).to_broadcast([P, 2, NC]),
+                    op=ALU.subtract,
                 )
-            s_ps[(r, b)] = s
-            if b == 0:
-                cp = m_pool.tile([P, 512], F32, name="c0")
-                nc.scalar.copy(out=cp[:], in_=s[:])
-                c0[r] = cp
-            t = t_pool.tile([P, 512], F32, name="tanh")
-            nc.scalar.activation(out=t[:], in_=s[:], func=ACT.Tanh, scale=0.5)
-            tanh[(r, b)] = t
 
-        def gate_and_max(r, b):
-            s = s_ps[(r, b)]
-            y = y_pool.tile([P, 512], F32, name="y")
-            nc.vector.scalar_tensor_tensor(out=y[:], in0=tanh[(r, b)][:], scalar=1.0, in1=s[:], op0=ALU.add, op1=ALU.mult)
-            yv[(r, b)] = y
-            if b == 1:
-                mx[r] = m_pool.tile([P, 512], F32, name="mx")
-                nc.vector.tensor_tensor(out=mx[r][:], in0=s[:], in1=c0[r][:], op=ALU.max)
-            elif b > 1:
-                nc.vector.tensor_tensor(out=mx[r][:], in0=s[:], in1=mx[r][:], op=ALU.max)
-            if b == BANKS - 1:
-                mm[r] = m_pool.tile([P, NC], F32, name="mm")
-                nc.vector.tensor_tensor(out=mm[r][:], in0=mx[r][:, 0:NC], in1=mx[r][:, NC : 2 * NC], op=ALU.max)
+        def gates(hb, c):
+            d = d_of[(hb, c)]
+            y = y_of[(hb, c)]
+            for cols in (slice(B, 4 * B), slice(0, B)):
+                nc.scalar.activation(out=d[:, cols], in_=d[:, cols], func=ACT.Exp)
+            for cols in (slice(1 * B, 2 * B), slice(2 * B, 3 * B), slice(3 * B, 4 * B), slice(0, B)):
+                nc.gpsimd.tensor_tensor(out=y[:, cols], in0=y[:, cols], in1=d[:, cols], op=ALU.mult)
 
-        def weights(r, b):
-            s = s_ps[(r, b)]
-            d = u_pool.tile([P, 512], F32, name="u")
-            nc.vector.tensor_tensor(
-                out=d[:].rearrange("p (a n) -> p a n", a=2),
-                in0=s[:].rearrange("p (a n) -> p a n", a=2),
-                in1=mm[r][:].unsqueeze(1).to_broadcast([P, 2, NC]),
-                op=ALU.subtract,
-            )
-            nc.scalar.activation(out=d[:], in_=d[:], func=ACT.Exp)
-            du[(r, b)] = d
-            y = yv[(r, b)]
-            nc.gpsimd.tensor_tensor(out=y[:], in0=y[:], in1=d[:], op=ALU.mult)
+        z_of = {}
 
-        def sums(r):
-            z = ps_za.tile([P, 512], F32, name="za")
+        def sums(hb, c):
+            z = ps_t.tile([P, B], F32, name="t")
             for slot in range(4):
-                src = du if slot < 2 else yv
+                src = d_of[(hb, c)] if slot < 2 else y_of[(hb, c)]
                 nb = slot % 2
                 for w in range(W):
                     nc.tensor.matmul(
                         out=z[:, slot * P : (slot + 1) * P],
-                        lhsT=src[(r, w // 2)][:, (w % 2) * NC + nb * P : (w % 2) * NC + (nb + 1) * P],
+                        lhsT=src[:, w * NC + nb * P : w * NC + (nb + 1) * P],
                         rhs=ident[:],
                         is_transpose=True,
                         start=(w == 0),
                         stop=(w == W - 1),
                     )
-            za[r] = z
+            z_of[(hb, c)] = z
 
-        def finish(r):
-            hb, c = r // 2, r % 2
-            z = za[r]
-            rz = m_pool.tile([P, NC], F32, name="rz")
+        def finish(hb, c):
+            z = z_of[(hb, c)]
+            g = hb // 2
+            if g not in o_of:
+                o_of[g] = o_pool.tile([P, N // P, COLS], F32, name="o")
+            rz = m_pool.tile([P, NC], F32, name="rz", bufs=2)
             nc.vector.reciprocal(out=rz[:], in_=z[:, 0:NC])
-            nc.vector.scalar_tensor_tensor(
-                out=out_sb[:, 2 * c : 2 * c + 2, hb * P : (hb + 1) * P],
+            nc.vector.tensor_tensor(
+                out=o_of[g][:, 2 * c : 2 * c + 2, (hb % 2) * P : (hb % 2 + 1) * P],
                 in0=z[:, NC : 2 * NC].rearrange("p (a h) -> p a h", a=2),
-                scalar=0.5,
                 in1=rz[:].rearrange("p (a h) -> p a h", a=2),
-                op0=ALU.mult,
-                op1=ALU.mult,
+                op=ALU.mult,
             )
-            if hb % 4 == 3 and c == 1:
-                cols = slice((hb - 3) * P, (hb + 1) * P)
-                for nb in range(N // P):
-                    nc.sync.dma_start(out=out[nb * P : (nb + 1) * P, cols], in_=out_sb[:, nb, cols])
 
-        HEAD = 6
-        for i in range(HEAD):
-            load(i)
-        for i in range(HEAD):
+        def prepare(i, engines):
             for j in range(4):
-                transposes(i, j, "scalar" if j % 2 == 0 else "vector")
-            load(i + HEAD)
-            if i > 0:
-                quantise(i - 1)
-        quantise(HEAD - 1)
+                transposes(i, j, engines[j])
+            quantise(i)
 
-        for r in range(-1, ROUNDS + 1):
-            nxt = r + 1 < ROUNDS
-            if nxt:
-                fill(r + 1, 0)
-            hb_t = (r + 4) // 2
-            i_t = hb_t + 4
-            if r >= 0 and hb_t < H // P:
-                for j in range(2):
-                    transposes(i_t, 2 * (r % 2) + j, "scalar")
-                if r % 2 == 1 and i_t + HEAD < len(blocks):
-                    load(i_t + HEAD)
-            if 0 <= r < ROUNDS:
-                for b in range(BANKS):
-                    gate_and_max(r, b)
-            if r >= 1:
-                sums(r - 1)
-            for b in range(BANKS):
-                if 0 <= r < ROUNDS:
-                    weights(r, b)
-                if nxt and b < BANKS - 1:
-                    fill(r + 1, b + 1)
-            if r >= 1:
-                finish(r - 1)
-            hb_q = (r + 2) // 2
-            if r >= 2 and r % 2 == 0 and hb_q < H // P:
-                quantise(hb_q + 4)
+        AHEAD = 3
+        for i in range(AHEAD):
+            load(i)
+        for i in range(4):
+            prepare(i, ("scalar", "vector", "scalar", "vector"))
+            load(i + AHEAD)
+
+        def store(g):
+            for nb in range(N // P):
+                nc.sync.dma_start(out=out[nb * P : (nb + 1) * P, g * COLS : (g + 1) * COLS], in_=o_of[g][:, nb, :])
+
+        rounds = [[(2 * g + h, c) for c in range(2) for h in range(2)] for g in range(BATCHES)]
+        scores(*rounds[0][0])
+        shifts(*rounds[0][0])
+        for g in range(BATCHES):
+            silus(*rounds[g][0])
+            for k in range(4):
+                if g == 0 and k < 2:
+                    prepare(index[("x", 2 + k)], ("scalar", "vector", "scalar", "vector"))
+                    load(index[("x", 2 + k)] + AHEAD)
+                if k < 3:
+                    scores(*rounds[g][k + 1])
+                    silus(*rounds[g][k + 1])
+                if k < 3:
+                    shifts(*rounds[g][k + 1])
+                if g + 1 < BATCHES:
+                    i = index[("t", 2 * g + 2 + k // 2)]
+                    for j in range(2 * (k % 2), 2 * (k % 2) + 2):
+                        transposes(i, j, "scalar")
+                    if k % 2 == 1:
+                        quantise(i)
+                        if i + AHEAD < len(blocks):
+                            load(i + AHEAD)
+            if g + 1 < BATCHES:
+                scores(*rounds[g + 1][0])
+                shifts(*rounds[g + 1][0])
+            for k in range(4):
+                gates(*rounds[g][k])
+                if g > 0:
+                    sums(*rounds[g - 1][k])
+                    finish(*rounds[g - 1][k])
+            if g > 0:
+                store(g - 1)
+        for k in range(4):
+            sums(*rounds[BATCHES - 1][k])
+            finish(*rounds[BATCHES - 1][k])
+        store(BATCHES - 1)

@@ -21,6 +21,7 @@ BANKS = 4
 B = 512
 BATCHES = 8
 COLS = 2 * P
+AHEAD = 3
 
 
 def tile_dendriticlayersilu_ffn_kernel(tc, x, template_flat, out):
@@ -28,13 +29,13 @@ def tile_dendriticlayersilu_ffn_kernel(tc, x, template_flat, out):
     with ExitStack() as ctx:
         ctx.enter_context(tc.manual_schedule())
         const = ctx.enter_context(tc.tile_pool(name="const", bufs=1))
-        raw_pool = ctx.enter_context(tc.tile_pool(name="raw", bufs=3))
+        raw_pool = ctx.enter_context(tc.tile_pool(name="raw", bufs=AHEAD))
         grp_pool = ctx.enter_context(tc.tile_pool(name="grp", bufs=2))
         tq_pool = ctx.enter_context(tc.tile_pool(name="tq", bufs=4))
         c_pool = ctx.enter_context(tc.tile_pool(name="c", bufs=4))
         d_pool = ctx.enter_context(tc.tile_pool(name="d", bufs=8))
         y_pool = ctx.enter_context(tc.tile_pool(name="y", bufs=8))
-        m_pool = ctx.enter_context(tc.tile_pool(name="m", bufs=4))
+        m_pool = ctx.enter_context(tc.tile_pool(name="m", bufs=2))
         o_pool = ctx.enter_context(tc.tile_pool(name="o", bufs=2))
         ps_s = ctx.enter_context(tc.psum_pool(name="ps_s", bufs=5))
         ps_t = ctx.enter_context(tc.psum_pool(name="ps_t", bufs=3))
@@ -46,25 +47,38 @@ def tile_dendriticlayersilu_ffn_kernel(tc, x, template_flat, out):
         xq = const.tile([P, W * N], U32, name="xq", align_bytes=64)
         xs = const.tile([P, W * N], U8, name="xs", align_bytes=64)
 
-        blocks = [("x", 0), ("x", 1), ("t", 0), ("t", 1), ("x", 2), ("x", 3)] + [("t", i) for i in range(2, H // P)]
+        blocks = [("x", 0), ("t", 0), ("x", 1), ("t", 1), ("x", 2), ("x", 3)] + [("t", i) for i in range(2, H // P)]
         index = {block: i for i, block in enumerate(blocks)}
         raw = {}
         grp = {}
         tq = {}
         ts = {}
+        latest = []
 
         def load(i):
+            if i >= len(blocks):
+                return
             kind, idx = blocks[i]
             src = x if kind == "x" else template_flat
             r = raw_pool.tile([P, W * K], BF16, name="raw")
             nc.sync.dma_start(out=r[:], in_=src[idx * P : (idx + 1) * P, :])
             raw[i] = r
 
-        def transposes(i, j, engine):
+        def scratch_matmuls(bank, count):
+            for n in range(count):
+                nc.tensor.matmul(out=bank[:, 0:P], lhsT=ident[:], rhs=ident[:], start=True, stop=True)
+
+        def scratch_passes(bank, count):
+            for w in range(count):
+                one_pass(latest[-1], 0, w, bank[:, 0:NC])
+
+        def transposes(i, j, engine, scratch=None, count=0):
             if j == 0:
                 grp[i] = grp_pool.tile([P, W * K], BF16, name="grp", align_bytes=64)
             words = raw[i][:].bitcast(F32)
             tp = ps_t.tile([P, B], F32, name="t")
+            if scratch is not None:
+                scratch(tp, count)
             for q in range(4):
                 first = (2 * j + q // 2) * 2 * P + q % 2
                 nc.tensor.transpose(tp[:, q * P : (q + 1) * P], words[:, first : first + 2 * P - 1 : 2], ident[:])
@@ -92,26 +106,30 @@ def tile_dendriticlayersilu_ffn_kernel(tc, x, template_flat, out):
         d_of = {}
         y_of = {}
         o_of = {}
-
         s_of = {}
         c_of = {}
+        z_of = {}
+        rz_of = {}
+
+        def one_pass(hb, c, w, dst):
+            cols = slice(w * N + c * NC, w * N + (c + 1) * NC)
+            nc.tensor.matmul_mx(
+                out=dst,
+                lhsT=tq[hb][:, w * P : (w + 1) * P].bitcast(FP8X4),
+                lhsT_scale=ts[hb][:, w * P : (w + 1) * P],
+                rhs=xq[:, cols].bitcast(FP8X4),
+                rhs_scale=xs[:, cols],
+                start=True,
+                stop=True,
+            )
 
         def scores(hb, c):
+            latest.append(hb)
             banks = []
             for b in range(BANKS):
                 s = ps_s.tile([P, B], F32, name="s")
                 for a in range(2):
-                    w = 2 * b + a
-                    cols = slice(w * N + c * NC, w * N + (c + 1) * NC)
-                    nc.tensor.matmul_mx(
-                        out=s[:, a * NC : (a + 1) * NC],
-                        lhsT=tq[hb][:, w * P : (w + 1) * P].bitcast(FP8X4),
-                        lhsT_scale=ts[hb][:, w * P : (w + 1) * P],
-                        rhs=xq[:, cols].bitcast(FP8X4),
-                        rhs_scale=xs[:, cols],
-                        start=True,
-                        stop=True,
-                    )
+                    one_pass(hb, c, 2 * b + a, s[:, a * NC : (a + 1) * NC])
                 banks.append(s)
                 if b == 0:
                     c0 = c_pool.tile([P, B], F32, name="c0")
@@ -130,10 +148,11 @@ def tile_dendriticlayersilu_ffn_kernel(tc, x, template_flat, out):
             c0 = c_of[(hb, c)]
             d = d_pool.tile([P, BANKS * B], F32, name="d")
             d_of[(hb, c)] = d
-            mx = m_pool.tile([P, B], F32, name="mx", bufs=2)
-            nc.vector.tensor_tensor(out=mx[:], in0=banks[1][:], in1=c0[:], op=ALU.max)
-            for b in range(2, BANKS):
-                nc.vector.tensor_tensor(out=mx[:], in0=banks[b][:], in1=mx[:], op=ALU.max)
+            mx = m_pool.tile([P, B], F32, name="mx")
+            for b in range(1, BANKS):
+                for a in range(2):
+                    cols = slice(a * NC, (a + 1) * NC)
+                    nc.vector.tensor_tensor(out=mx[:, cols], in0=banks[b][:, cols], in1=(c0 if b == 1 else mx)[:, cols], op=ALU.max)
             mm = m_pool.tile([P, NC], F32, name="mm")
             nc.vector.tensor_reduce(out=mm[:], in_=mx[:].rearrange("p (a n) -> p n a", a=2), op=ALU.max, axis=AX.X)
             for b in list(range(1, BANKS)) + [0]:
@@ -145,18 +164,19 @@ def tile_dendriticlayersilu_ffn_kernel(tc, x, template_flat, out):
                     op=ALU.subtract,
                 )
 
-        def gates(hb, c):
+        def gates(hb, c, engine):
             d = d_of[(hb, c)]
             y = y_of[(hb, c)]
             for cols in (slice(B, 4 * B), slice(0, B)):
                 nc.scalar.activation(out=d[:, cols], in_=d[:, cols], func=ACT.Exp)
-            for cols in (slice(1 * B, 2 * B), slice(2 * B, 3 * B), slice(3 * B, 4 * B), slice(0, B)):
-                nc.gpsimd.tensor_tensor(out=y[:, cols], in0=y[:, cols], in1=d[:, cols], op=ALU.mult)
+            for b in (1, 2, 3, 0):
+                cols = slice(b * B, (b + 1) * B)
+                engine.tensor_tensor(out=y[:, cols], in0=y[:, cols], in1=d[:, cols], op=ALU.mult)
 
-        z_of = {}
-
-        def sums(hb, c):
+        def sums(hb, c, count=2):
             z = ps_t.tile([P, B], F32, name="t")
+            z_of[(hb, c)] = z
+            scratch_passes(z, count)
             for slot in range(4):
                 src = d_of[(hb, c)] if slot < 2 else y_of[(hb, c)]
                 nb = slot % 2
@@ -169,71 +189,94 @@ def tile_dendriticlayersilu_ffn_kernel(tc, x, template_flat, out):
                         start=(w == 0),
                         stop=(w == W - 1),
                     )
-            z_of[(hb, c)] = z
 
-        def finish(hb, c):
-            z = z_of[(hb, c)]
+        def invert(hb, c):
+            rz = m_pool.tile([P, NC], F32, name="rz")
+            rz_of[(hb, c)] = rz
+            nc.vector.reciprocal(out=rz[:], in_=z_of[(hb, c)][:, 0:NC])
+
+        def normalise(hb, c):
             g = hb // 2
             if g not in o_of:
                 o_of[g] = o_pool.tile([P, N // P, COLS], F32, name="o")
-            rz = m_pool.tile([P, NC], F32, name="rz", bufs=2)
-            nc.vector.reciprocal(out=rz[:], in_=z[:, 0:NC])
             nc.vector.tensor_tensor(
                 out=o_of[g][:, 2 * c : 2 * c + 2, (hb % 2) * P : (hb % 2 + 1) * P],
-                in0=z[:, NC : 2 * NC].rearrange("p (a h) -> p a h", a=2),
-                in1=rz[:].rearrange("p (a h) -> p a h", a=2),
+                in0=z_of[(hb, c)][:, NC : 2 * NC].rearrange("p (a h) -> p a h", a=2),
+                in1=rz_of[(hb, c)][:].rearrange("p (a h) -> p a h", a=2),
                 op=ALU.mult,
             )
-
-        def prepare(i, engines):
-            for j in range(4):
-                transposes(i, j, engines[j])
-            quantise(i)
-
-        AHEAD = 3
-        for i in range(AHEAD):
-            load(i)
-        for i in range(4):
-            prepare(i, ("scalar", "vector", "scalar", "vector"))
-            load(i + AHEAD)
 
         def store(g):
             for nb in range(N // P):
                 nc.sync.dma_start(out=out[nb * P : (nb + 1) * P, g * COLS : (g + 1) * COLS], in_=o_of[g][:, nb, :])
 
+        def prepare(i, count, engines):
+            for j in range(4):
+                transposes(i, j, engines[j % 2], scratch_matmuls, count)
+            load(i + AHEAD)
+
+        for i in range(AHEAD):
+            load(i)
+        pre = ps_t.tile([P, B], F32, name="t")
+        scratch_matmuls(pre, 6)
+        for i in range(3):
+            prepare(i, 1, ("scalar", "vector"))
+            quantise(i)
+        prepare(3, 1, ("scalar", "scalar"))
+
         rounds = [[(2 * g + h, c) for c in range(2) for h in range(2)] for g in range(BATCHES)]
         scores(*rounds[0][0])
+        silus(*rounds[0][0])
+        quantise(3)
+        prepare(4, 0, ("scalar", "scalar"))
         shifts(*rounds[0][0])
         for g in range(BATCHES):
-            silus(*rounds[g][0])
+            if g > 0:
+                silus(*rounds[g][0])
             for k in range(4):
-                if g == 0 and k < 2:
-                    prepare(index[("x", 2 + k)], ("scalar", "vector", "scalar", "vector"))
-                    load(index[("x", 2 + k)] + AHEAD)
+                if g == 0 and k == 1:
+                    quantise(5)
                 if k < 3:
                     scores(*rounds[g][k + 1])
                     silus(*rounds[g][k + 1])
-                if k < 3:
+                    if g == 0 and k == 0:
+                        quantise(4)
+                        prepare(5, 0, ("scalar", "scalar"))
                     shifts(*rounds[g][k + 1])
-                if g + 1 < BATCHES:
+                if g + 1 == BATCHES:
+                    sums(*rounds[g - 1][k], 4)
+                    invert(*rounds[g - 1][k])
+                    if k > 0:
+                        normalise(*rounds[g - 1][k - 1])
+                    if k == 3:
+                        normalise(*rounds[g - 1][3])
+                        store(g - 1)
+                if g + 1 < BATCHES and (g > 0 or k > 0):
                     i = index[("t", 2 * g + 2 + k // 2)]
-                    for j in range(2 * (k % 2), 2 * (k % 2) + 2):
-                        transposes(i, j, "scalar")
+                    for j in range(0 if g == 0 and k == 1 else 2 * (k % 2), 2 * (k % 2) + 2):
+                        transposes(i, j, "scalar", scratch_passes, 4 if j % 2 == 0 else 0)
                     if k % 2 == 1:
                         quantise(i)
-                        if i + AHEAD < len(blocks):
-                            load(i + AHEAD)
+                        load(i + AHEAD)
             if g + 1 < BATCHES:
                 scores(*rounds[g + 1][0])
                 shifts(*rounds[g + 1][0])
+            last = g + 1 == BATCHES
             for k in range(4):
-                gates(*rounds[g][k])
-                if g > 0:
+                gates(*rounds[g][k], nc.gpsimd if not last or k < 1 else nc.vector)
+                if g > 0 and not last:
                     sums(*rounds[g - 1][k])
-                    finish(*rounds[g - 1][k])
-            if g > 0:
+                    invert(*rounds[g - 1][k])
+                    if k > 0:
+                        normalise(*rounds[g - 1][k - 1])
+                if last:
+                    sums(*rounds[g][k], 4)
+                    if k > 0:
+                        invert(*rounds[g][k - 1])
+                        normalise(*rounds[g][k - 1])
+            if g > 0 and not last:
+                normalise(*rounds[g - 1][3])
                 store(g - 1)
-        for k in range(4):
-            sums(*rounds[BATCHES - 1][k])
-            finish(*rounds[BATCHES - 1][k])
+        invert(*rounds[BATCHES - 1][3])
+        normalise(*rounds[BATCHES - 1][3])
         store(BATCHES - 1)

@@ -68,9 +68,9 @@ def tile_dendriticlayersilu_ffn_kernel(tc, x, template_flat, out):
             for n in range(count):
                 nc.tensor.matmul(out=bank[:, 0:P], lhsT=ident[:], rhs=ident[:], start=True, stop=True)
 
-        def scratch_passes(bank, count):
+        def scratch_passes(bank, count, first=0):
             for w in range(count):
-                one_pass(latest[-1], 0, w, bank[:, 0:NC])
+                one_pass(latest[-1], 0, w % W, bank[:, first : first + NC])
 
         def transposes(i, j, engine, scratch=None, count=0):
             if j == 0:
@@ -178,6 +178,8 @@ def tile_dendriticlayersilu_ffn_kernel(tc, x, template_flat, out):
             z_of[(hb, c)] = z
             scratch_passes(z, count)
             for slot in range(4):
+                if slot == 2:
+                    scratch_passes(z, count, NC)
                 src = d_of[(hb, c)] if slot < 2 else y_of[(hb, c)]
                 nb = slot % 2
                 for w in range(W):
@@ -254,7 +256,7 @@ def tile_dendriticlayersilu_ffn_kernel(tc, x, template_flat, out):
                 if g + 1 < BATCHES and (g > 0 or k > 0):
                     i = index[("t", 2 * g + 2 + k // 2)]
                     for j in range(0 if g == 0 and k == 1 else 2 * (k % 2), 2 * (k % 2) + 2):
-                        transposes(i, j, "scalar", scratch_passes, 4 if j % 2 == 0 else 0)
+                        transposes(i, j, "scalar", scratch_passes, 2)
                     if k % 2 == 1:
                         quantise(i)
                         load(i + AHEAD)

from contextlib import ExitStack

import concourse.mybir as mybir
from concourse.masks import make_identity

FP8X4 = mybir.dt.float8_e4m3fn_x4
BF16 = mybir.dt.bfloat16
F32 = mybir.dt.float32
U32 = mybir.dt.uint32
U8 = mybir.dt.uint8
ACT = mybir.ActivationFunctionType
ALU = mybir.AluOpType
AX = mybir.AxisListType

P = 128
N, H, W, K = 512, 2048, 8, 512
FLOPS = 2 * N * H * W * K

NC = 256
BANKS = 4
B = 512
BATCHES = 8
COLS = 2 * P
AHEAD = 3


def tile_dendriticlayersilu_ffn_kernel(tc, x, template_flat, out):
    nc = tc.nc
    with ExitStack() as ctx:
        ctx.enter_context(tc.manual_schedule())
        const = ctx.enter_context(tc.tile_pool(name="const", bufs=1))
        raw_pool = ctx.enter_context(tc.tile_pool(name="raw", bufs=AHEAD))
        grp_pool = ctx.enter_context(tc.tile_pool(name="grp", bufs=2))
        tq_pool = ctx.enter_context(tc.tile_pool(name="tq", bufs=4))
        c_pool = ctx.enter_context(tc.tile_pool(name="c", bufs=4))
        d_pool = ctx.enter_context(tc.tile_pool(name="d", bufs=8))
        y_pool = ctx.enter_context(tc.tile_pool(name="y", bufs=8))
        m_pool = ctx.enter_context(tc.tile_pool(name="m", bufs=2))
        o_pool = ctx.enter_context(tc.tile_pool(name="o", bufs=2))
        ps_s = ctx.enter_context(tc.psum_pool(name="ps_s", bufs=5))
        ps_t = ctx.enter_context(tc.psum_pool(name="ps_t", bufs=3))

        ident = const.tile([P, P], F32, name="ident")
        make_identity(nc, ident[:])
        warm = const.tile([P, 1], F32, name="warm")
        nc.scalar.activation(out=warm[:], in_=ident[:, 0:1], func=ACT.Silu)
        xq = const.tile([P, W * N], U32, name="xq", align_bytes=64)
        xs = const.tile([P, W * N], U8, name="xs", align_bytes=64)

        blocks = [("x", 0), ("t", 0), ("x", 1), ("t", 1), ("x", 2), ("x", 3)] + [("t", i) for i in range(2, H // P)]
        index = {block: i for i, block in enumerate(blocks)}
        raw = {}
        grp = {}
        tq = {}
        ts = {}
        latest = []

        def load(i):
            if i >= len(blocks):
                return
            kind, idx = blocks[i]
            src = x if kind == "x" else template_flat
            r = raw_pool.tile([P, W * K], BF16, name="raw")
            nc.sync.dma_start(out=r[:], in_=src[idx * P : (idx + 1) * P, :])
            raw[i] = r

        def scratch_matmuls(bank, count):
            for n in range(count):
                nc.tensor.matmul(out=bank[:, 0:P], lhsT=ident[:], rhs=ident[:], start=True, stop=True)

        def scratch_passes(bank, count, first=0):
            for w in range(count):
                one_pass(latest[-1], 0, w % W, bank[:, first : first + NC])

        def transposes(i, j, engine, scratch=None, count=0):
            if j == 0:
                grp[i] = grp_pool.tile([P, W * K], BF16, name="grp", align_bytes=64)
            words = raw[i][:].bitcast(F32)
            tp = ps_t.tile([P, B], F32, name="t")
            if scratch is not None:
                scratch(tp, count)
            for q in range(4):
                first = (2 * j + q // 2) * 2 * P + q % 2
                nc.tensor.transpose(tp[:, q * P : (q + 1) * P], words[:, first : first + 2 * P - 1 : 2], ident[:])
            dst = grp[i][:].bitcast(F32)[:, j * B : (j + 1) * B].rearrange("p (a r u) -> p a r u", a=2, u=2)
            src = tp[:].rearrange("p (a u r) -> p a r u", a=2, u=2)
            if engine == "scalar":
                nc.scalar.copy(out=dst, in_=src)
            else:
                nc.vector.tensor_copy(out=dst, in_=src)

        def quantise(i):
            kind, idx = blocks[i]
            g = grp[i]
            if kind == "x":
                for w in range(W):
                    cols = slice(w * N + idx * P, w * N + (idx + 1) * P)
                    nc.vector.quantize_mx(out=xq[:, cols].bitcast(FP8X4), scales=xs[:, cols], in_=g[:, w * K : (w + 1) * K])
            else:
                q = tq_pool.tile([P, W * P], U32, name="tq", align_bytes=64)
                s = tq_pool.tile([P, W * P], U8, name="ts", align_bytes=64)
                nc.vector.quantize_mx(out=q[:].bitcast(FP8X4), scales=s[:], in_=g[:])
                tq[idx] = q
                ts[idx] = s

        d_of = {}
        y_of = {}
        o_of = {}
        s_of = {}
        c_of = {}
        z_of = {}
        rz_of = {}

        def one_pass(hb, c, w, dst):
            cols = slice(w * N + c * NC, w * N + (c + 1) * NC)
            nc.tensor.matmul_mx(
                out=dst,
                lhsT=tq[hb][:, w * P : (w + 1) * P].bitcast(FP8X4),
                lhsT_scale=ts[hb][:, w * P : (w + 1) * P],
                rhs=xq[:, cols].bitcast(FP8X4),
                rhs_scale=xs[:, cols],
                start=True,
                stop=True,
            )

        def scores(hb, c):
            latest.append(hb)
            banks = []
            for b in range(BANKS):
                s = ps_s.tile([P, B], F32, name="s")
                for a in range(2):
                    one_pass(hb, c, 2 * b + a, s[:, a * NC : (a + 1) * NC])
                banks.append(s)
                if b == 0:
                    c0 = c_pool.tile([P, B], F32, name="c0")
                    nc.scalar.copy(out=c0[:], in_=s[:])
                    c_of[(hb, c)] = c0
            s_of[(hb, c)] = banks

        def silus(hb, c):
            y = y_pool.tile([P, BANKS * B], F32, name="y")
            y_of[(hb, c)] = y
            for b in range(BANKS):
                nc.scalar.activation(out=y[:, b * B : (b + 1) * B], in_=s_of[(hb, c)][b][:], func=ACT.Silu)

        def shifts(hb, c):
            banks = s_of[(hb, c)]
            c0 = c_of[(hb, c)]
            d = d_pool.tile([P, BANKS * B], F32, name="d")
            d_of[(hb, c)] = d
            mx = m_pool.tile([P, B], F32, name="mx")
            for b in range(1, BANKS):
                for a in range(2):
                    cols = slice(a * NC, (a + 1) * NC)
                    nc.vector.tensor_tensor(out=mx[:, cols], in0=banks[b][:, cols], in1=(c0 if b == 1 else mx)[:, cols], op=ALU.max)
            mm = m_pool.tile([P, NC], F32, name="mm")
            nc.vector.tensor_reduce(out=mm[:], in_=mx[:].rearrange("p (a n) -> p n a", a=2), op=ALU.max, axis=AX.X)
            for b in list(range(1, BANKS)) + [0]:
                engine, source = (nc.gpsimd, c0) if b == 0 else (nc.vector, banks[b])
                engine.tensor_tensor(
                    out=d[:, b * B : (b + 1) * B].rearrange("p (a n) -> p a n", a=2),
                    in0=source[:].rearrange("p (a n) -> p a n", a=2),
                    in1=mm[:].unsqueeze(1).to_broadcast([P, 2, NC]),
                    op=ALU.subtract,
                )

        def gates(hb, c, engine):
            d = d_of[(hb, c)]
            y = y_of[(hb, c)]
            for cols in (slice(B, 4 * B), slice(0, B)):
                nc.scalar.activation(out=d[:, cols], in_=d[:, cols], func=ACT.Exp)
            for b in (1, 2, 3, 0):
                cols = slice(b * B, (b + 1) * B)
                engine.tensor_tensor(out=y[:, cols], in0=y[:, cols], in1=d[:, cols], op=ALU.mult)

        def sums(hb, c, count=2):
            z = ps_t.tile([P, B], F32, name="t")
            z_of[(hb, c)] = z
            scratch_passes(z, count)
            for slot in range(4):
                if slot == 2:
                    scratch_passes(z, count, NC)
                src = d_of[(hb, c)] if slot < 2 else y_of[(hb, c)]
                nb = slot % 2
                for w in range(W):
                    nc.tensor.matmul(
                        out=z[:, slot * P : (slot + 1) * P],
                        lhsT=src[:, w * NC + nb * P : w * NC + (nb + 1) * P],
                        rhs=ident[:],
                        is_transpose=True,
                        start=(w == 0),
                        stop=(w == W - 1),
                    )

        def invert(hb, c):
            rz = m_pool.tile([P, NC], F32, name="rz")
            rz_of[(hb, c)] = rz
            nc.vector.reciprocal(out=rz[:], in_=z_of[(hb, c)][:, 0:NC])

        def normalise(hb, c):
            g = hb // 2
            if g not in o_of:
                o_of[g] = o_pool.tile([P, N // P, COLS], F32, name="o")
            nc.vector.tensor_tensor(
                out=o_of[g][:, 2 * c : 2 * c + 2, (hb % 2) * P : (hb % 2 + 1) * P],
                in0=z_of[(hb, c)][:, NC : 2 * NC].rearrange("p (a h) -> p a h", a=2),
                in1=rz_of[(hb, c)][:].rearrange("p (a h) -> p a h", a=2),
                op=ALU.mult,
            )

        def store(g):
            for nb in range(N // P):
                nc.sync.dma_start(out=out[nb * P : (nb + 1) * P, g * COLS : (g + 1) * COLS], in_=o_of[g][:, nb, :])

        def prepare(i, count, engines):
            for j in range(4):
                transposes(i, j, engines[j % 2], scratch_matmuls, count)
            load(i + AHEAD)

        for i in range(AHEAD):
            load(i)
        pre = ps_t.tile([P, B], F32, name="t")
        scratch_matmuls(pre, 6)
        for i in range(3):
            prepare(i, 1, ("scalar", "vector"))
            quantise(i)
        prepare(3, 1, ("scalar", "scalar"))

        rounds = [[(2 * g + h, c) for c in range(2) for h in range(2)] for g in range(BATCHES)]
        scores(*rounds[0][0])
        silus(*rounds[0][0])
        quantise(3)
        prepare(4, 0, ("scalar", "scalar"))
        shifts(*rounds[0][0])
        for g in range(BATCHES):
            if g > 0:
                silus(*rounds[g][0])
            for k in range(4):
                if g == 0 and k == 1:
                    quantise(5)
                if k < 3:
                    scores(*rounds[g][k + 1])
                    silus(*rounds[g][k + 1])
                    if g == 0 and k == 0:
                        quantise(4)
                        prepare(5, 0, ("scalar", "scalar"))
                    shifts(*rounds[g][k + 1])
                if g + 1 == BATCHES:
                    sums(*rounds[g - 1][k], 4)
                    invert(*rounds[g - 1][k])
                    if k > 0:
                        normalise(*rounds[g - 1][k - 1])
                    if k == 3:
                        normalise(*rounds[g - 1][3])
                        store(g - 1)
                if g + 1 < BATCHES and (g > 0 or k > 0):
                    i = index[("t", 2 * g + 2 + k // 2)]
                    for j in range(0 if g == 0 and k == 1 else 2 * (k % 2), 2 * (k % 2) + 2):
                        transposes(i, j, "scalar", scratch_passes, 2)
                    if k % 2 == 1:
                        quantise(i)
                        load(i + AHEAD)
            if g + 1 < BATCHES:
                scores(*rounds[g + 1][0])
                shifts(*rounds[g + 1][0])
            last = g + 1 == BATCHES
            for k in range(4):
                gates(*rounds[g][k], nc.gpsimd if not last or k < 1 else nc.vector)
                if g > 0 and not last:
                    sums(*rounds[g - 1][k])
                    invert(*rounds[g - 1][k])
                    if k > 0:
                        normalise(*rounds[g - 1][k - 1])
                if last:
                    sums(*rounds[g][k], 4)
                    if k > 0:
                        invert(*rounds[g][k - 1])
                        normalise(*rounds[g][k - 1])
            if g > 0 and not last:
                normalise(*rounds[g - 1][3])
                store(g - 1)
        invert(*rounds[BATCHES - 1][3])
        normalise(*rounds[BATCHES - 1][3])
        store(BATCHES - 1)
